import numpy as np
import ml_dtypes


def mxq(x, axis, fmt="e4m3"):
    dtype, down = {"e4m3": (ml_dtypes.float8_e4m3fn, 7), "e5m2": (ml_dtypes.float8_e5m2, 14)}[fmt]
    v = np.moveaxis(np.asarray(x, np.float32).astype(ml_dtypes.bfloat16).astype(np.float64), axis, -1)
    blocks = v.reshape(v.shape[:-1] + (-1, 32))
    amax = np.abs(blocks).max(-1, keepdims=True)
    byte = np.maximum(np.where(amax > 0, np.frexp(amax)[1] - 1 + 127, 0) - down, 1)
    scale = np.exp2(byte - 127.0)
    codes = (blocks / scale).astype(np.float32).astype(dtype).astype(np.float64)
    return np.moveaxis((codes * scale).reshape(v.shape), -1, axis)


WIDE = False


def mx_kscale(k):
    if not WIDE:
        return np.ones(k)
    levels = np.array([10, -10, 5, -5, 0])
    a = np.random.permutation(np.resize(levels, k // 512 * 4)).reshape(k // 512, 4)
    idx = np.arange(k)
    return np.exp2(a[idx // 512, idx % 128 // 32])


BF16 = ml_dtypes.bfloat16


def bf(x):
    return np.asarray(x, np.float32).astype(BF16)


def f64(x):
    return np.asarray(x).astype(np.float64)


ND, NS, D0, D1, D2, D3, DH, C = 2048, 2048, 512, 128, 256, 512, 256, 10
SIG = 4.0


def draw_adj():
    w = np.exp(SIG * np.random.standard_normal((ND, NS)))
    return w / w.sum(1, keepdims=True)


def setup_inputs():
    u = mx_kscale(NS)
    return {"x1": bf(np.maximum(np.random.standard_normal((NS, D1)), 0.0) / u[:, None]),
            "adj": bf(draw_adj() * u),
            "W1": bf(np.random.standard_normal((D1, D2)) * 2.0 / np.sqrt(D1)),
            "b1": bf(np.random.standard_normal(D2) * 0.5 / u.max())}


def reference(x1, adj, W1, b1):
    h = f64(x1) @ f64(W1) + f64(b1)
    return np.maximum(mxq(f64(adj), 1, "e4m3") @ mxq(h, 0, "e4m3"), 0.0)

@@ -1,0 +1,169 @@
+from contextlib import ExitStack
+
+import concourse.mybir as mybir
+from concourse.masks import make_identity
+
+F32 = mybir.dt.float32
+BF16 = mybir.dt.bfloat16
+U32 = mybir.dt.uint32
+U8 = mybir.dt.uint8
+FP8X4 = mybir.dt.float8_e4m3fn_x4
+
+P = 128
+PACK = 4
+K_PASS = P * PACK
+BANK = 512
+
+N_DST, N_SRC, D_IN, D_OUT = 2048, 2048, 128, 256
+PASSES = N_SRC // K_PASS
+DST_TILES = N_DST // P
+SLOTS = PASSES * PACK
+WORDS = N_SRC // 2
+ROUND = 2
+ROUNDS = DST_TILES // ROUND
+LEAD = 2
+assert PASSES == LEAD * ROUND
+
+FLOPS = 2 * N_DST * N_SRC * D_OUT + 2 * N_SRC * D_IN * D_OUT
+
+
+def tile_gcn_pb_kernel(tc, x1, adj, W1, b1, out):
+    nc = tc.nc
+    with ExitStack() as ctx:
+        ctx.enter_context(tc.manual_schedule())
+        keep = ctx.enter_context(tc.tile_pool(name="keep", bufs=1))
+        stage = ctx.enter_context(tc.tile_pool(name="stage", bufs=6))
+        psum_t = ctx.enter_context(tc.psum_pool(name="psum_t", bufs=6))
+        psum_mm = ctx.enter_context(tc.psum_pool(name="psum_mm", bufs=2))
+
+        bias_rows = keep.tile([P, D_OUT], BF16, name="bias_rows")
+        nc.vector.memset(bias_rows[:], 0.0)
+        nc.sync.dma_start(out=bias_rows[0:1, :], in_=b1.rearrange("(o f) -> o f", o=1))
+        w1_sb = keep.tile([P, D_OUT], BF16, name="w1_sb")
+        nc.sync.dma_start(out=w1_sb[:], in_=W1)
+        x1_sb = keep.tile([P, SLOTS * D_IN], BF16, name="x1_sb")
+        nc.sync.dma_start(
+            out=x1_sb[:].rearrange("p (c w) -> p c w", w=2 * D_IN),
+            in_=x1.rearrange("(c p e) d -> p c (e d)", p=P, e=2),
+        )
+        adj_rows = adj.rearrange("(p a) k -> p (a k)", a=DST_TILES)
+        adj_sb = []
+        for r in range(ROUNDS):
+            adj_r = keep.tile([P, ROUND * N_SRC], BF16, name="adj%d" % r)
+            nc.sync.dma_start(
+                out=adj_r[:], in_=adj_rows[:, r * ROUND * N_SRC : (r + 1) * ROUND * N_SRC]
+            )
+            adj_sb.append(adj_r)
+
+        ident_bf = keep.tile([P, P], BF16, name="ident_bf")
+        make_identity(nc, ident_bf[:])
+        ident_f32 = keep.tile([P, P], F32, name="ident_f32")
+        make_identity(nc, ident_f32[:])
+        ones = keep.tile([P, P], BF16, name="ones")
+        nc.vector.memset(ones[:], 1.0)
+
+        bias_ps = psum_mm.tile([P, D_OUT], F32, tag="mm")
+        nc.tensor.matmul(out=bias_ps[:], lhsT=ones[:], rhs=bias_rows[:], start=True, stop=True)
+        bias_all = keep.tile([P, D_OUT], F32, name="bias_all")
+        nc.vector.tensor_copy(out=bias_all[:], in_=bias_ps[:])
+
+        x1T = keep.tile([P, SLOTS * P], BF16, name="x1T")
+        for j in range(SLOTS // PACK):
+            x1T_ps = psum_t.tile([P, PACK * P], BF16, tag="t")
+            for t in range(PACK):
+                s = PACK * j + t
+                nc.tensor.transpose(
+                    x1T_ps[:, t * P : (t + 1) * P], x1_sb[:, s * D_IN : (s + 1) * D_IN], ident_bf[:]
+                )
+            nc.scalar.copy(out=x1T[:, j * PACK * P : (j + 1) * PACK * P], in_=x1T_ps[:])
+
+        h_grouped = keep.tile([P, PASSES * D_OUT * PACK], BF16, name="h_grouped", align_bytes=64)
+        h_grouped_v = h_grouped[:].rearrange("p (g f t) -> p g f t", g=PASSES, t=PACK)
+
+        def h_pass(g):
+            for f0 in range(0, D_OUT, P):
+                h_ps = psum_mm.tile([P, BANK], F32, tag="mm")
+                for t in range(PACK):
+                    s = PACK * g + t
+                    nc.tensor.matmul(
+                        out=h_ps[:, t * P : (t + 1) * P],
+                        lhsT=x1T[:, s * P : (s + 1) * P],
+                        rhs=w1_sb[:, f0 : f0 + P],
+                        start=True,
+                        stop=True,
+                    )
+                nc.vector.tensor_tensor(
+                    out=h_grouped_v[:, g, f0 : f0 + P, :],
+                    in0=h_ps[:].rearrange("p (t f) -> p f t", t=PACK),
+                    in1=bias_all[:, f0 : f0 + P].unsqueeze(2).to_broadcast([P, P, PACK]),
+                    op=mybir.AluOpType.add,
+                )
+
+        grouped = {}
+        codes = {}
+
+        def transpose_tile(a):
+            adj_words = adj_sb[a // ROUND][:].bitcast(F32)
+            first = (a % ROUND) * WORDS
+            grouped[a] = stage.tile([P, N_SRC], BF16, name="grouped", align_bytes=64)
+            grouped_words = grouped[a][:].bitcast(F32)
+            for b in range(WORDS // BANK):
+                adjT_ps = psum_t.tile([P, BANK], F32, tag="t")
+                for j in range(BANK // P):
+                    w0 = first + b * BANK + j * P
+                    nc.tensor.transpose(
+                        adjT_ps[:, j * P : (j + 1) * P], adj_words[:, w0 : w0 + P], ident_f32[:]
+                    )
+                nc.scalar.copy(
+                    out=grouped_words[:, b * BANK : (b + 1) * BANK].rearrange(
+                        "p (g i u) -> p g i u", i=P, u=2
+                    ),
+                    in_=adjT_ps[:].rearrange("p (g u i) -> p g i u", i=P, u=2),
+                )
+
+        def quantise_tile(a):
+            packed = stage.tile([P, PASSES * P], U32, name="adj_packed", align_bytes=64)
+            scales = stage.tile([P, PASSES * P], U8, name="adj_scales", align_bytes=64)
+            nc.vector.quantize_mx(out=packed[:].bitcast(FP8X4), scales=scales[:], in_=grouped[a][:])
+            codes[a] = (packed, scales)
+
+        def multiply_tile(a, acc):
+            packed, scales = codes[a]
+            for g in range(PASSES):
+                nc.tensor.matmul_mx(
+                    out=acc,
+                    lhsT=packed[:, g * P : (g + 1) * P].bitcast(FP8X4),
+                    lhsT_scale=scales[:, g * P : (g + 1) * P],
+                    rhs=h_packed[:, g * D_OUT : (g + 1) * D_OUT].bitcast(FP8X4),
+                    rhs_scale=h_scales[:, g * D_OUT : (g + 1) * D_OUT],
+                    start=(g == 0),
+                    stop=(g == PASSES - 1),
+                )
+
+        def tiles_of(r):
+            return range(r * ROUND, (r + 1) * ROUND)
+
+        for g in range(PASSES):
+            h_pass(g)
+            transpose_tile(g)
+        h_packed = keep.tile([P, PASSES * D_OUT], U32, name="h_packed", align_bytes=64)
+        h_scales = keep.tile([P, PASSES * D_OUT], U8, name="h_scales", align_bytes=64)
+        nc.vector.quantize_mx(out=h_packed[:].bitcast(FP8X4), scales=h_scales[:], in_=h_grouped[:])
+        for a in tiles_of(0):
+            quantise_tile(a)
+
+        out_sb = keep.tile([P, DST_TILES * D_OUT], F32, name="out_sb")
+        out_rows = out.rearrange("(p a) f -> p (a f)", a=DST_TILES)
+        for r in range(ROUNDS):
+            if r + LEAD < ROUNDS:
+                for a in tiles_of(r + LEAD):
+                    transpose_tile(a)
+            if r + 1 < ROUNDS:
+                for a in tiles_of(r + 1):
+                    quantise_tile(a)
+            acc = psum_mm.tile([P, BANK], F32, tag="mm")
+            for a in tiles_of(r):
+                multiply_tile(a, acc[:, (a % ROUND) * D_OUT : (a % ROUND + 1) * D_OUT])
+            cols = slice(r * BANK, (r + 1) * BANK)
+            nc.vector.tensor_scalar_max(out=out_sb[:, cols], in0=acc[:], scalar1=0.0)
+            nc.sync.dma_start(out=out_rows[:, cols], in_=out_sb[:, cols])

@@ -21,8 +21,8 @@ SLOTS = PASSES * PACK
 WORDS = N_SRC // 2
 ROUND = 2
 ROUNDS = DST_TILES // ROUND
-LEAD = 2
-assert PASSES == LEAD * ROUND
+BUNCH = 2
+assert PASSES == BUNCH * ROUND
 
 FLOPS = 2 * N_DST * N_SRC * D_OUT + 2 * N_SRC * D_IN * D_OUT
 
@@ -32,7 +32,7 @@ def tile_gcn_pb_kernel(tc, x1, adj, W1, b1, out):
     with ExitStack() as ctx:
         ctx.enter_context(tc.manual_schedule())
         keep = ctx.enter_context(tc.tile_pool(name="keep", bufs=1))
-        stage = ctx.enter_context(tc.tile_pool(name="stage", bufs=6))
+        stage = ctx.enter_context(tc.tile_pool(name="stage", bufs=2 * BUNCH * ROUND))
         psum_t = ctx.enter_context(tc.psum_pool(name="psum_t", bufs=6))
         psum_mm = ctx.enter_context(tc.psum_pool(name="psum_mm", bufs=2))
 
@@ -149,21 +149,23 @@ def tile_gcn_pb_kernel(tc, x1, adj, W1, b1, out):
         h_packed = keep.tile([P, PASSES * D_OUT], U32, name="h_packed", align_bytes=64)
         h_scales = keep.tile([P, PASSES * D_OUT], U8, name="h_scales", align_bytes=64)
         nc.vector.quantize_mx(out=h_packed[:].bitcast(FP8X4), scales=h_scales[:], in_=h_grouped[:])
-        for a in tiles_of(0):
-            quantise_tile(a)
+        for r in range(BUNCH):
+            for a in tiles_of(r):
+                quantise_tile(a)
 
         out_sb = keep.tile([P, DST_TILES * D_OUT], F32, name="out_sb")
         out_rows = out.rearrange("(p a) f -> p (a f)", a=DST_TILES)
-        for r in range(ROUNDS):
-            if r + LEAD < ROUNDS:
-                for a in tiles_of(r + LEAD):
+        for first in range(0, ROUNDS, BUNCH):
+            for r in range(first + BUNCH, min(first + 2 * BUNCH, ROUNDS)):
+                for a in tiles_of(r):
                     transpose_tile(a)
-            if r + 1 < ROUNDS:
-                for a in tiles_of(r + 1):
-                    quantise_tile(a)
-            acc = psum_mm.tile([P, BANK], F32, tag="mm")
-            for a in tiles_of(r):
-                multiply_tile(a, acc[:, (a % ROUND) * D_OUT : (a % ROUND + 1) * D_OUT])
-            cols = slice(r * BANK, (r + 1) * BANK)
-            nc.vector.tensor_scalar_max(out=out_sb[:, cols], in0=acc[:], scalar1=0.0)
-            nc.sync.dma_start(out=out_rows[:, cols], in_=out_sb[:, cols])
+            for r in range(first, first + BUNCH):
+                if r + BUNCH < ROUNDS:
+                    for a in tiles_of(r + BUNCH):
+                        quantise_tile(a)
+                acc = psum_mm.tile([P, BANK], F32, tag="mm")
+                for a in tiles_of(r):
+                    multiply_tile(a, acc[:, (a % ROUND) * D_OUT : (a % ROUND + 1) * D_OUT])
+                cols = slice(r * BANK, (r + 1) * BANK)
+                nc.vector.tensor_scalar_max(out=out_sb[:, cols], in0=acc[:], scalar1=0.0)
+                nc.sync.dma_start(out=out_rows[:, cols], in_=out_sb[:, cols])

@@ -33,19 +33,19 @@ def tile_gcn_pb_kernel(tc, x1, adj, W1, b1, out):
         ctx.enter_context(tc.manual_schedule())
         keep = ctx.enter_context(tc.tile_pool(name="keep", bufs=1))
         stage = ctx.enter_context(tc.tile_pool(name="stage", bufs=2 * BUNCH * ROUND))
-        psum_t = ctx.enter_context(tc.psum_pool(name="psum_t", bufs=6))
-        psum_mm = ctx.enter_context(tc.psum_pool(name="psum_mm", bufs=2))
+        psum_t = ctx.enter_context(tc.psum_pool(name="psum_t", bufs=5))
+        psum_mm = ctx.enter_context(tc.psum_pool(name="psum_mm", bufs=3))
 
+        x1_sb = keep.tile([P, SLOTS * D_IN], BF16, name="x1_sb")
+        x1_sb_v = x1_sb[:].rearrange("p (c w) -> p c w", w=2 * D_IN)
+        x1_v = x1.rearrange("(c p e) d -> p c (e d)", p=P, e=2)
+        for g in range(PASSES):
+            nc.sync.dma_start(out=x1_sb_v[:, 2 * g : 2 * g + 2, :], in_=x1_v[:, 2 * g : 2 * g + 2, :])
+        w1_sb = keep.tile([P, D_OUT], BF16, name="w1_sb")
+        nc.sync.dma_start(out=w1_sb[:], in_=W1)
         bias_rows = keep.tile([P, D_OUT], BF16, name="bias_rows")
         nc.vector.memset(bias_rows[:], 0.0)
         nc.sync.dma_start(out=bias_rows[0:1, :], in_=b1.rearrange("(o f) -> o f", o=1))
-        w1_sb = keep.tile([P, D_OUT], BF16, name="w1_sb")
-        nc.sync.dma_start(out=w1_sb[:], in_=W1)
-        x1_sb = keep.tile([P, SLOTS * D_IN], BF16, name="x1_sb")
-        nc.sync.dma_start(
-            out=x1_sb[:].rearrange("p (c w) -> p c w", w=2 * D_IN),
-            in_=x1.rearrange("(c p e) d -> p c (e d)", p=P, e=2),
-        )
         adj_rows = adj.rearrange("(p a) k -> p (a k)", a=DST_TILES)
         adj_sb = []
         for r in range(ROUNDS):
@@ -62,11 +62,6 @@ def tile_gcn_pb_kernel(tc, x1, adj, W1, b1, out):
         ones = keep.tile([P, P], BF16, name="ones")
         nc.vector.memset(ones[:], 1.0)
 
-        bias_ps = psum_mm.tile([P, D_OUT], F32, tag="mm")
-        nc.tensor.matmul(out=bias_ps[:], lhsT=ones[:], rhs=bias_rows[:], start=True, stop=True)
-        bias_all = keep.tile([P, D_OUT], F32, name="bias_all")
-        nc.vector.tensor_copy(out=bias_all[:], in_=bias_ps[:])
-
         x1T = keep.tile([P, SLOTS * P], BF16, name="x1T")
         for j in range(SLOTS // PACK):
             x1T_ps = psum_t.tile([P, PACK * P], BF16, tag="t")
@@ -76,6 +71,11 @@ def tile_gcn_pb_kernel(tc, x1, adj, W1, b1, out):
                     x1T_ps[:, t * P : (t + 1) * P], x1_sb[:, s * D_IN : (s + 1) * D_IN], ident_bf[:]
                 )
             nc.scalar.copy(out=x1T[:, j * PACK * P : (j + 1) * PACK * P], in_=x1T_ps[:])
+
+        bias_ps = psum_mm.tile([P, D_OUT], F32, tag="mm")
+        nc.tensor.matmul(out=bias_ps[:], lhsT=ones[:], rhs=bias_rows[:], start=True, stop=True)
+        bias_all = keep.tile([P, D_OUT], F32, name="bias_all")
+        nc.vector.tensor_copy(out=bias_all[:], in_=bias_ps[:])
 
         h_grouped = keep.tile([P, PASSES * D_OUT * PACK], BF16, name="h_grouped", align_bytes=64)
         h_grouped_v = h_grouped[:].rearrange("p (g f t) -> p g f t", g=PASSES, t=PACK)

from contextlib import ExitStack

import concourse.mybir as mybir
from concourse.masks import make_identity

F32 = mybir.dt.float32
BF16 = mybir.dt.bfloat16
U32 = mybir.dt.uint32
U8 = mybir.dt.uint8
FP8X4 = mybir.dt.float8_e4m3fn_x4

P = 128
PACK = 4
K_PASS = P * PACK
BANK = 512

N_DST, N_SRC, D_IN, D_OUT = 2048, 2048, 128, 256
PASSES = N_SRC // K_PASS
DST_TILES = N_DST // P
SLOTS = PASSES * PACK
WORDS = N_SRC // 2
ROUND = 2
ROUNDS = DST_TILES // ROUND
BUNCH = 2
assert PASSES == BUNCH * ROUND

FLOPS = 2 * N_DST * N_SRC * D_OUT + 2 * N_SRC * D_IN * D_OUT


def tile_gcn_pb_kernel(tc, x1, adj, W1, b1, out):
    nc = tc.nc
    with ExitStack() as ctx:
        ctx.enter_context(tc.manual_schedule())
        keep = ctx.enter_context(tc.tile_pool(name="keep", bufs=1))
        stage = ctx.enter_context(tc.tile_pool(name="stage", bufs=2 * BUNCH * ROUND))
        psum_t = ctx.enter_context(tc.psum_pool(name="psum_t", bufs=5))
        psum_mm = ctx.enter_context(tc.psum_pool(name="psum_mm", bufs=3))

        x1_sb = keep.tile([P, SLOTS * D_IN], BF16, name="x1_sb")
        x1_sb_v = x1_sb[:].rearrange("p (c w) -> p c w", w=2 * D_IN)
        x1_v = x1.rearrange("(c p e) d -> p c (e d)", p=P, e=2)
        for g in range(PASSES):
            nc.sync.dma_start(out=x1_sb_v[:, 2 * g : 2 * g + 2, :], in_=x1_v[:, 2 * g : 2 * g + 2, :])
        w1_sb = keep.tile([P, D_OUT], BF16, name="w1_sb")
        nc.sync.dma_start(out=w1_sb[:], in_=W1)
        bias_rows = keep.tile([P, D_OUT], BF16, name="bias_rows")
        nc.vector.memset(bias_rows[:], 0.0)
        nc.sync.dma_start(out=bias_rows[0:1, :], in_=b1.rearrange("(o f) -> o f", o=1))
        adj_rows = adj.rearrange("(p a) k -> p (a k)", a=DST_TILES)
        adj_sb = []
        for r in range(ROUNDS):
            adj_r = keep.tile([P, ROUND * N_SRC], BF16, name="adj%d" % r)
            nc.sync.dma_start(
                out=adj_r[:], in_=adj_rows[:, r * ROUND * N_SRC : (r + 1) * ROUND * N_SRC]
            )
            adj_sb.append(adj_r)

        ident_bf = keep.tile([P, P], BF16, name="ident_bf")
        make_identity(nc, ident_bf[:])
        ident_f32 = keep.tile([P, P], F32, name="ident_f32")
        make_identity(nc, ident_f32[:])
        ones = keep.tile([P, P], BF16, name="ones")
        nc.vector.memset(ones[:], 1.0)

        x1T = keep.tile([P, SLOTS * P], BF16, name="x1T")
        for j in range(SLOTS // PACK):
            x1T_ps = psum_t.tile([P, PACK * P], BF16, tag="t")
            for t in range(PACK):
                s = PACK * j + t
                nc.tensor.transpose(
                    x1T_ps[:, t * P : (t + 1) * P], x1_sb[:, s * D_IN : (s + 1) * D_IN], ident_bf[:]
                )
            nc.scalar.copy(out=x1T[:, j * PACK * P : (j + 1) * PACK * P], in_=x1T_ps[:])

        bias_ps = psum_mm.tile([P, D_OUT], F32, tag="mm")
        nc.tensor.matmul(out=bias_ps[:], lhsT=ones[:], rhs=bias_rows[:], start=True, stop=True)
        bias_all = keep.tile([P, D_OUT], F32, name="bias_all")
        nc.vector.tensor_copy(out=bias_all[:], in_=bias_ps[:])

        h_grouped = keep.tile([P, PASSES * D_OUT * PACK], BF16, name="h_grouped", align_bytes=64)
        h_grouped_v = h_grouped[:].rearrange("p (g f t) -> p g f t", g=PASSES, t=PACK)

        def h_pass(g):
            for f0 in range(0, D_OUT, P):
                h_ps = psum_mm.tile([P, BANK], F32, tag="mm")
                for t in range(PACK):
                    s = PACK * g + t
                    nc.tensor.matmul(
                        out=h_ps[:, t * P : (t + 1) * P],
                        lhsT=x1T[:, s * P : (s + 1) * P],
                        rhs=w1_sb[:, f0 : f0 + P],
                        start=True,
                        stop=True,
                    )
                nc.vector.tensor_tensor(
                    out=h_grouped_v[:, g, f0 : f0 + P, :],
                    in0=h_ps[:].rearrange("p (t f) -> p f t", t=PACK),
                    in1=bias_all[:, f0 : f0 + P].unsqueeze(2).to_broadcast([P, P, PACK]),
                    op=mybir.AluOpType.add,
                )

        grouped = {}
        codes = {}

        def transpose_tile(a):
            adj_words = adj_sb[a // ROUND][:].bitcast(F32)
            first = (a % ROUND) * WORDS
            grouped[a] = stage.tile([P, N_SRC], BF16, name="grouped", align_bytes=64)
            grouped_words = grouped[a][:].bitcast(F32)
            for b in range(WORDS // BANK):
                adjT_ps = psum_t.tile([P, BANK], F32, tag="t")
                for j in range(BANK // P):
                    w0 = first + b * BANK + j * P
                    nc.tensor.transpose(
                        adjT_ps[:, j * P : (j + 1) * P], adj_words[:, w0 : w0 + P], ident_f32[:]
                    )
                nc.scalar.copy(
                    out=grouped_words[:, b * BANK : (b + 1) * BANK].rearrange(
                        "p (g i u) -> p g i u", i=P, u=2
                    ),
                    in_=adjT_ps[:].rearrange("p (g u i) -> p g i u", i=P, u=2),
                )

        def quantise_tile(a):
            packed = stage.tile([P, PASSES * P], U32, name="adj_packed", align_bytes=64)
            scales = stage.tile([P, PASSES * P], U8, name="adj_scales", align_bytes=64)
            nc.vector.quantize_mx(out=packed[:].bitcast(FP8X4), scales=scales[:], in_=grouped[a][:])
            codes[a] = (packed, scales)

        def multiply_tile(a, acc):
            packed, scales = codes[a]
            for g in range(PASSES):
                nc.tensor.matmul_mx(
                    out=acc,
                    lhsT=packed[:, g * P : (g + 1) * P].bitcast(FP8X4),
                    lhsT_scale=scales[:, g * P : (g + 1) * P],
                    rhs=h_packed[:, g * D_OUT : (g + 1) * D_OUT].bitcast(FP8X4),
                    rhs_scale=h_scales[:, g * D_OUT : (g + 1) * D_OUT],
                    start=(g == 0),
                    stop=(g == PASSES - 1),
                )

        def tiles_of(r):
            return range(r * ROUND, (r + 1) * ROUND)

        for g in range(PASSES):
            h_pass(g)
            transpose_tile(g)
        h_packed = keep.tile([P, PASSES * D_OUT], U32, name="h_packed", align_bytes=64)
        h_scales = keep.tile([P, PASSES * D_OUT], U8, name="h_scales", align_bytes=64)
        nc.vector.quantize_mx(out=h_packed[:].bitcast(FP8X4), scales=h_scales[:], in_=h_grouped[:])
        for r in range(BUNCH):
            for a in tiles_of(r):
                quantise_tile(a)

        out_sb = keep.tile([P, DST_TILES * D_OUT], F32, name="out_sb")
        out_rows = out.rearrange("(p a) f -> p (a f)", a=DST_TILES)
        for first in range(0, ROUNDS, BUNCH):
            for r in range(first + BUNCH, min(first + 2 * BUNCH, ROUNDS)):
                for a in tiles_of(r):
                    transpose_tile(a)
            for r in range(first, first + BUNCH):
                if r + BUNCH < ROUNDS:
                    for a in tiles_of(r + BUNCH):
                        quantise_tile(a)
                acc = psum_mm.tile([P, BANK], F32, tag="mm")
                for a in tiles_of(r):
                    multiply_tile(a, acc[:, (a % ROUND) * D_OUT : (a % ROUND + 1) * D_OUT])
                cols = slice(r * BANK, (r + 1) * BANK)
                nc.vector.tensor_scalar_max(out=out_sb[:, cols], in0=acc[:], scalar1=0.0)
                nc.sync.dma_start(out=out_rows[:, cols], in_=out_sb[:, cols])
